import numpy as np
import ml_dtypes

BF16 = ml_dtypes.bfloat16


def bf(x):
    return np.asarray(x, np.float32).astype(BF16)


def f32(x):
    return np.asarray(x, np.float32)


def f64(x):
    return np.asarray(x).astype(np.float64)


def striped(idx):
    return np.tile(idx.reshape(-1, 16).T, (8, 1))


DIM, C, S, N = 256, 512, 512, 256
EPS = 1e-05


def setup_inputs():
    return {"x": f32(np.random.standard_normal((DIM, N))), "nw": f32(1.0 + 0.1 * np.random.standard_normal((DIM, 1))), "wkv": bf(np.random.standard_normal((DIM, C)) / np.sqrt(DIM)), "base": f32(np.random.standard_normal((C, S))), "offs": striped(np.random.permutation(S)[:N])}


def reference(x, nw, wkv, base, offs):
    idx = offs[:16].T.reshape(-1)
    xx = f64(x)
    r = 1.0 / np.sqrt(np.mean(xx * xx, axis=0, keepdims=True) + EPS)
    p = f64(wkv).T @ (f64(nw) * xx)
    out = f64(base).copy()
    out[:, idx] = p * r
    return out

@@ -1,0 +1,73 @@
+import concourse.mybir as mybir
+
+P = 128
+DIM, C, S, N = 256, 512, 512, 256
+D_BLOCKS = DIM // P
+C_BLOCKS = C // P
+EPS = 1e-05
+
+FLOPS = 2 * DIM * C * N + 2 * DIM * N
+
+F32, BF16, U16 = mybir.dt.float32, mybir.dt.bfloat16, mybir.dt.uint16
+ACT = mybir.ActivationFunctionType
+MULT = mybir.AluOpType.mult
+
+
+def tile_pagedtransformerblock_kernel(tc, x, nw, wkv, base, offs, out):
+    nc = tc.nc
+    with (
+        tc.tile_pool(name="held", bufs=1) as held,
+        tc.psum_pool(name="psum", bufs=1) as psum,
+    ):
+        offsets = held.tile([P, N // 16], U16, name="offsets")
+        nc.sync.dma_start(offsets[:], offs)
+
+        gain = held.tile([P, D_BLOCKS], F32, name="gain")
+        with nc.allow_non_contiguous_dma(reason="256 gains, one to a partition"):
+            nc.scalar.dma_start(gain[:], nw.rearrange("(k p) o -> p (k o)", p=P))
+
+        x_blocks = [held.tile([P, N], F32, name=f"x{k}") for k in range(D_BLOCKS)]
+        nc.sync.dma_start(x_blocks[0][:], x[0:P, :])
+        nc.scalar.dma_start(x_blocks[1][:], x[P : 2 * P, :])
+
+        weights = held.tile([P, D_BLOCKS, C], BF16, name="weights")
+        nc.sync.dma_start(weights[:], wkv.rearrange("(k p) c -> p k c", p=P))
+
+        windows = [held.tile([P, S], F32, name=f"window{b}") for b in range(C_BLOCKS)]
+        for b in range(C_BLOCKS):
+            queue = nc.scalar if b % 2 == 0 else nc.sync
+            queue.dma_start(windows[b][:], base[b * P : (b + 1) * P, :])
+
+        averager = held.tile([P, P], BF16, name="averager")
+        nc.gpsimd.memset(averager[:], 1.0 / DIM)
+        eps = held.tile([P, 1], F32, name="eps")
+        nc.gpsimd.memset(eps[:], EPS)
+
+        mean_sq = psum.tile([P, N], F32, name="mean_sq")
+        for k in range(D_BLOCKS):
+            squares = held.tile([P, N], BF16, name=f"squares{k}")
+            nc.scalar.activation(squares[:], x_blocks[k][:], ACT.Square)
+            nc.tensor.matmul(
+                mean_sq[:], averager[:], squares[:], start=(k == 0), stop=(k == D_BLOCKS - 1)
+            )
+        r = held.tile([P, N], F32, name="r")
+        nc.scalar.activation(r[:], mean_sq[:], ACT.Abs_reciprocal_sqrt, bias=eps[:])
+
+        scaled = [held.tile([P, N], BF16, name=f"scaled{k}") for k in range(D_BLOCKS)]
+        for k in range(D_BLOCKS):
+            nc.vector.tensor_scalar_mul(scaled[k][:], x_blocks[k][:], gain[:, k : k + 1])
+
+        for b in range(C_BLOCKS):
+            p = psum.tile([P, N], F32, name=f"p{b}")
+            for k in range(D_BLOCKS):
+                nc.tensor.matmul(
+                    p[:],
+                    weights[:, k, b * P : (b + 1) * P],
+                    scaled[k][:],
+                    start=(k == 0),
+                    stop=(k == D_BLOCKS - 1),
+                )
+            product = held.tile([P, N], F32, name=f"product{b}")
+            nc.scalar.copy(product[:], p[:])
+            nc.vector.tensor_tensor(windows[b][:].indirect(offsets[:]), product[:], r[:], MULT)
+            nc.sync.dma_start(out[b * P : (b + 1) * P, :], windows[b][:])

@@ -43,6 +43,9 @@ def tile_pagedtransformerblock_kernel(tc, x, nw, wkv, base, offs, out):
         eps = held.tile([P, 1], F32, name="eps")
         nc.gpsimd.memset(eps[:], EPS)
 
+        warm = held.tile([P, 1], F32, name="warm")
+        nc.scalar.activation(warm[:], eps[:], ACT.Abs_reciprocal_sqrt)
+
         mean_sq = psum.tile([P, N], F32, name="mean_sq")
         for k in range(D_BLOCKS):
             squares = held.tile([P, N], BF16, name=f"squares{k}")

@@ -19,46 +19,46 @@ def tile_pagedtransformerblock_kernel(tc, x, nw, wkv, base, offs, out):
         tc.tile_pool(name="held", bufs=1) as held,
         tc.psum_pool(name="psum", bufs=1) as psum,
     ):
-        offsets = held.tile([P, N // 16], U16, name="offsets")
-        nc.sync.dma_start(offsets[:], offs)
+        x_all = held.tile([P, D_BLOCKS, N], F32, name="x_all")
+        nc.sync.dma_start(x_all[:], x.rearrange("(k p) j -> p k j", p=P))
+        x_blocks = [x_all[:, k, :] for k in range(D_BLOCKS)]
 
         gain = held.tile([P, D_BLOCKS], F32, name="gain")
         with nc.allow_non_contiguous_dma(reason="256 gains, one to a partition"):
-            nc.scalar.dma_start(gain[:], nw.rearrange("(k p) o -> p (k o)", p=P))
-
-        x_blocks = [held.tile([P, N], F32, name=f"x{k}") for k in range(D_BLOCKS)]
-        nc.sync.dma_start(x_blocks[0][:], x[0:P, :])
-        nc.scalar.dma_start(x_blocks[1][:], x[P : 2 * P, :])
+            nc.sync.dma_start(gain[:], nw.rearrange("(k p) o -> p (k o)", p=P))
 
         weights = held.tile([P, D_BLOCKS, C], BF16, name="weights")
         nc.sync.dma_start(weights[:], wkv.rearrange("(k p) c -> p k c", p=P))
 
+        offsets = held.tile([P, N // 16], U16, name="offsets")
+        nc.sync.dma_start(offsets[:], offs)
+
         windows = [held.tile([P, S], F32, name=f"window{b}") for b in range(C_BLOCKS)]
         for b in range(C_BLOCKS):
-            queue = nc.scalar if b % 2 == 0 else nc.sync
-            queue.dma_start(windows[b][:], base[b * P : (b + 1) * P, :])
+            nc.sync.dma_start(windows[b][:], base[b * P : (b + 1) * P, :])
 
-        averager = held.tile([P, P], BF16, name="averager")
-        nc.gpsimd.memset(averager[:], 1.0 / DIM)
         eps = held.tile([P, 1], F32, name="eps")
-        nc.gpsimd.memset(eps[:], EPS)
+        nc.vector.memset(eps[:], EPS)
+        averager = held.tile([P, P], BF16, name="averager")
+        nc.vector.memset(averager[:], 1.0 / DIM)
 
         warm = held.tile([P, 1], F32, name="warm")
         nc.scalar.activation(warm[:], eps[:], ACT.Abs_reciprocal_sqrt)
 
+        squares = [held.tile([P, N], BF16, name=f"squares{k}") for k in range(D_BLOCKS)]
+        nc.vector.tensor_tensor(squares[0][:], x_blocks[0], x_blocks[0], MULT)
+        nc.scalar.activation(squares[1][:], x_blocks[1], ACT.Square)
         mean_sq = psum.tile([P, N], F32, name="mean_sq")
         for k in range(D_BLOCKS):
-            squares = held.tile([P, N], BF16, name=f"squares{k}")
-            nc.scalar.activation(squares[:], x_blocks[k][:], ACT.Square)
             nc.tensor.matmul(
-                mean_sq[:], averager[:], squares[:], start=(k == 0), stop=(k == D_BLOCKS - 1)
+                mean_sq[:], averager[:], squares[k][:], start=(k == 0), stop=(k == D_BLOCKS - 1)
             )
         r = held.tile([P, N], F32, name="r")
         nc.scalar.activation(r[:], mean_sq[:], ACT.Abs_reciprocal_sqrt, bias=eps[:])
 
         scaled = [held.tile([P, N], BF16, name=f"scaled{k}") for k in range(D_BLOCKS)]
-        for k in range(D_BLOCKS):
-            nc.vector.tensor_scalar_mul(scaled[k][:], x_blocks[k][:], gain[:, k : k + 1])
+        nc.vector.tensor_scalar_mul(scaled[0][:], x_blocks[0], gain[:, 0:1])
+        nc.scalar.activation(scaled[1][:], x_blocks[1], ACT.Identity, scale=gain[:, 1:2])
 
         for b in range(C_BLOCKS):
             p = psum.tile([P, N], F32, name=f"p{b}")

@@ -5,6 +5,7 @@ DIM, C, S, N = 256, 512, 512, 256
 D_BLOCKS = DIM // P
 C_BLOCKS = C // P
 EPS = 1e-05
+WARMING_MATMULS = 16
 
 FLOPS = 2 * DIM * C * N + 2 * DIM * N
 
@@ -44,6 +45,10 @@ def tile_pagedtransformerblock_kernel(tc, x, nw, wkv, base, offs, out):
 
         warm = held.tile([P, 1], F32, name="warm")
         nc.scalar.activation(warm[:], eps[:], ACT.Abs_reciprocal_sqrt)
+
+        unread = psum.tile([P, P], F32, name="unread")
+        for i in range(WARMING_MATMULS):
+            nc.tensor.matmul(unread[:], averager[:], averager[:], start=True, stop=True)
 
         squares = [held.tile([P, N], BF16, name=f"squares{k}") for k in range(D_BLOCKS)]
         nc.vector.tensor_tensor(squares[0][:], x_blocks[0], x_blocks[0], MULT)

@@ -21,15 +21,14 @@ def tile_pagedtransformerblock_kernel(tc, x, nw, wkv, base, offs, out):
         tc.psum_pool(name="psum", bufs=1) as psum,
     ):
         x_all = held.tile([P, D_BLOCKS, N], F32, name="x_all")
-        nc.sync.dma_start(x_all[:], x.rearrange("(k p) j -> p k j", p=P))
+        nc.sync.dma_start(x_all[:], x.rearrange("(p k) j -> p k j", p=P))
         x_blocks = [x_all[:, k, :] for k in range(D_BLOCKS)]
 
         gain = held.tile([P, D_BLOCKS], F32, name="gain")
-        with nc.allow_non_contiguous_dma(reason="256 gains, one to a partition"):
-            nc.sync.dma_start(gain[:], nw.rearrange("(k p) o -> p (k o)", p=P))
+        nc.sync.dma_start(gain[:], nw.rearrange("(p k) o -> p (k o)", p=P))
 
         weights = held.tile([P, D_BLOCKS, C], BF16, name="weights")
-        nc.sync.dma_start(weights[:], wkv.rearrange("(k p) c -> p k c", p=P))
+        nc.sync.dma_start(weights[:], wkv.rearrange("(p k) c -> p k c", p=P))
 
         offsets = held.tile([P, N // 16], U16, name="offsets")
         nc.sync.dma_start(offsets[:], offs)

@@ -49,22 +49,12 @@ def tile_pagedtransformerblock_kernel(tc, x, nw, wkv, base, offs, out):
         for i in range(WARMING_MATMULS):
             nc.tensor.matmul(unread[:], averager[:], averager[:], start=True, stop=True)
 
-        squares = [held.tile([P, N], BF16, name=f"squares{k}") for k in range(D_BLOCKS)]
-        nc.vector.tensor_tensor(squares[0][:], x_blocks[0], x_blocks[0], MULT)
-        nc.scalar.activation(squares[1][:], x_blocks[1], ACT.Square)
-        mean_sq = psum.tile([P, N], F32, name="mean_sq")
-        for k in range(D_BLOCKS):
-            nc.tensor.matmul(
-                mean_sq[:], averager[:], squares[k][:], start=(k == 0), stop=(k == D_BLOCKS - 1)
-            )
-        r = held.tile([P, N], F32, name="r")
-        nc.scalar.activation(r[:], mean_sq[:], ACT.Abs_reciprocal_sqrt, bias=eps[:])
 
         scaled = [held.tile([P, N], BF16, name=f"scaled{k}") for k in range(D_BLOCKS)]
-        nc.vector.tensor_scalar_mul(scaled[0][:], x_blocks[0], gain[:, 0:1])
-        nc.scalar.activation(scaled[1][:], x_blocks[1], ACT.Identity, scale=gain[:, 1:2])
+        for k in range(D_BLOCKS):
+            nc.vector.tensor_scalar_mul(scaled[k][:], x_blocks[k], gain[:, k : k + 1])
 
-        for b in range(C_BLOCKS):
+        def project(b):
             p = psum.tile([P, N], F32, name=f"p{b}")
             for k in range(D_BLOCKS):
                 nc.tensor.matmul(
@@ -76,5 +66,23 @@ def tile_pagedtransformerblock_kernel(tc, x, nw, wkv, base, offs, out):
                 )
             product = held.tile([P, N], F32, name=f"product{b}")
             nc.scalar.copy(product[:], p[:])
-            nc.vector.tensor_tensor(windows[b][:].indirect(offsets[:]), product[:], r[:], MULT)
+            return product
+
+        squares = [held.tile([P, N], BF16, name=f"squares{k}") for k in range(D_BLOCKS)]
+        nc.scalar.activation(squares[1][:], x_blocks[1], ACT.Square)
+        products = [project(0)]
+        nc.vector.tensor_tensor(squares[0][:], x_blocks[0], x_blocks[0], MULT)
+
+        mean_sq = psum.tile([P, N], F32, name="mean_sq")
+        for k in range(D_BLOCKS):
+            nc.tensor.matmul(
+                mean_sq[:], averager[:], squares[k][:], start=(k == 0), stop=(k == D_BLOCKS - 1)
+            )
+        r = held.tile([P, N], F32, name="r")
+        nc.scalar.activation(r[:], mean_sq[:], ACT.Abs_reciprocal_sqrt, bias=eps[:])
+
+        for b in range(C_BLOCKS):
+            if b + 1 < C_BLOCKS:
+                products.append(project(b + 1))
+            nc.vector.tensor_tensor(windows[b][:].indirect(offsets[:]), products[b][:], r[:], MULT)
             nc.sync.dma_start(out[b * P : (b + 1) * P, :], windows[b][:])

@@ -5,6 +5,7 @@ DIM, C, S, N = 256, 512, 512, 256
 D_BLOCKS = DIM // P
 C_BLOCKS = C // P
 EPS = 1e-05
+HALF = N // 2
 WARMING_MATMULS = 16
 
 FLOPS = 2 * DIM * C * N + 2 * DIM * N
@@ -49,40 +50,70 @@ def tile_pagedtransformerblock_kernel(tc, x, nw, wkv, base, offs, out):
         for i in range(WARMING_MATMULS):
             nc.tensor.matmul(unread[:], averager[:], averager[:], start=True, stop=True)
 
+        scaled = held.tile([P, D_BLOCKS, N], BF16, name="scaled")
+        squares = held.tile([P, D_BLOCKS, N], BF16, name="squares")
+        r = held.tile([P, N], F32, name="r")
+        halves = [slice(h * HALF, (h + 1) * HALF) for h in range(2)]
 
-        scaled = [held.tile([P, N], BF16, name=f"scaled{k}") for k in range(D_BLOCKS)]
-        for k in range(D_BLOCKS):
-            nc.vector.tensor_scalar_mul(scaled[k][:], x_blocks[k], gain[:, k : k + 1])
+        def scale(tokens):
+            for k in range(D_BLOCKS):
+                nc.vector.tensor_scalar_mul(
+                    scaled[:, k, tokens], x_all[:, k, tokens], gain[:, k : k + 1]
+                )
 
-        def project(b):
-            p = psum.tile([P, N], F32, name=f"p{b}")
+        def normalise(h):
+            mean_sq = psum.tile([P, HALF], F32, name=f"mean_sq{h}")
+            for k in range(D_BLOCKS):
+                nc.tensor.matmul(
+                    mean_sq[:],
+                    averager[:],
+                    squares[:, k, halves[h]],
+                    start=(k == 0),
+                    stop=(k == D_BLOCKS - 1),
+                )
+            nc.scalar.activation(r[:, halves[h]], mean_sq[:], ACT.Abs_reciprocal_sqrt, bias=eps[:])
+
+        def project(name, b, tokens, columns, bank):
+            p = psum.tile([P, columns], F32, name=f"p_{name}", tag=bank)
             for k in range(D_BLOCKS):
                 nc.tensor.matmul(
                     p[:],
                     weights[:, k, b * P : (b + 1) * P],
-                    scaled[k][:],
+                    scaled[:, k, tokens],
                     start=(k == 0),
                     stop=(k == D_BLOCKS - 1),
                 )
-            product = held.tile([P, N], F32, name=f"product{b}")
+            product = held.tile([P, columns], F32, name=f"product_{name}")
             nc.scalar.copy(product[:], p[:])
             return product
 
-        squares = [held.tile([P, N], BF16, name=f"squares{k}") for k in range(D_BLOCKS)]
-        nc.scalar.activation(squares[1][:], x_blocks[1], ACT.Square)
-        products = [project(0)]
-        nc.vector.tensor_tensor(squares[0][:], x_blocks[0], x_blocks[0], MULT)
-
-        mean_sq = psum.tile([P, N], F32, name="mean_sq")
-        for k in range(D_BLOCKS):
-            nc.tensor.matmul(
-                mean_sq[:], averager[:], squares[k][:], start=(k == 0), stop=(k == D_BLOCKS - 1)
+        def scatter_half(h, product):
+            lists = slice(h * HALF // 16, (h + 1) * HALF // 16)
+            nc.vector.tensor_tensor(
+                windows[0][:].indirect(offsets[:, lists]), product[:], r[:, halves[h]], MULT
             )
-        r = held.tile([P, N], F32, name="r")
-        nc.scalar.activation(r[:], mean_sq[:], ACT.Abs_reciprocal_sqrt, bias=eps[:])
 
-        for b in range(C_BLOCKS):
-            if b + 1 < C_BLOCKS:
-                products.append(project(b + 1))
-            nc.vector.tensor_tensor(windows[b][:].indirect(offsets[:]), products[b][:], r[:], MULT)
+        def scatter_block(b, product):
+            nc.vector.tensor_tensor(windows[b][:].indirect(offsets[:]), product[:], r[:], MULT)
+
+        def store(b):
             nc.sync.dma_start(out[b * P : (b + 1) * P, :], windows[b][:])
+
+        first, second = halves
+        nc.scalar.activation(squares[:, 1, first], x_all[:, 1, first], ACT.Square)
+        nc.vector.tensor_tensor(squares[:, 0, first], x_all[:, 0, first], x_all[:, 0, first], MULT)
+        scale(first)
+        normalise(0)
+        scatter_half(0, project("0a", 0, first, HALF, "bank_0a"))
+
+        scale(second)
+        nc.vector.tensor_tensor(squares[:, :, second], x_all[:, :, second], x_all[:, :, second], MULT)
+        normalise(1)
+
+        for b in (1, 2):
+            scatter_block(b, project(f"{b}", b, slice(0, N), N, f"bank_{b}"))
+            store(b)
+        scatter_half(1, project("0b", 0, second, HALF, "bank_2"))
+        store(0)
+        scatter_block(3, project("3", 3, slice(0, N), N, "bank_3"))
+        store(3)

@@ -21,12 +21,12 @@ def tile_pagedtransformerblock_kernel(tc, x, nw, wkv, base, offs, out):
         tc.tile_pool(name="held", bufs=1) as held,
         tc.psum_pool(name="psum", bufs=1) as psum,
     ):
+        gain = held.tile([P, D_BLOCKS], F32, name="gain")
+        nc.sync.dma_start(gain[:], nw.rearrange("(p k) o -> p (k o)", p=P))
+
         x_all = held.tile([P, D_BLOCKS, N], F32, name="x_all")
         nc.sync.dma_start(x_all[:], x.rearrange("(p k) j -> p k j", p=P))
         x_blocks = [x_all[:, k, :] for k in range(D_BLOCKS)]
-
-        gain = held.tile([P, D_BLOCKS], F32, name="gain")
-        nc.sync.dma_start(gain[:], nw.rearrange("(p k) o -> p (k o)", p=P))
 
         weights = held.tile([P, D_BLOCKS, C], BF16, name="weights")
         nc.sync.dma_start(weights[:], wkv.rearrange("(p k) c -> p k c", p=P))
@@ -107,7 +107,7 @@ def tile_pagedtransformerblock_kernel(tc, x, nw, wkv, base, offs, out):
         scatter_half(0, project("0a", 0, first, HALF, "bank_0a"))
 
         scale(second)
-        nc.vector.tensor_tensor(squares[:, :, second], x_all[:, :, second], x_all[:, :, second], MULT)
+        nc.scalar.activation(squares[:, :, second], x_all[:, :, second], ACT.Square)
         normalise(1)
 
         for b in (1, 2):

@@ -6,7 +6,9 @@ D_BLOCKS = DIM // P
 C_BLOCKS = C // P
 EPS = 1e-05
 HALF = N // 2
-WARMING_MATMULS = 16
+BANK = 512
+WARMING_MATMULS = 4
+WARM_ROWS = 32
 
 FLOPS = 2 * DIM * C * N + 2 * DIM * N
 
@@ -46,9 +48,13 @@ def tile_pagedtransformerblock_kernel(tc, x, nw, wkv, base, offs, out):
         warm = held.tile([P, 1], F32, name="warm")
         nc.scalar.activation(warm[:], eps[:], ACT.Abs_reciprocal_sqrt)
 
-        unread = psum.tile([P, P], F32, name="unread")
+        ones = held.tile([P, WARM_ROWS], BF16, name="ones")
+        nc.gpsimd.memset(ones[:], 1.0)
+        unread = psum.tile([WARM_ROWS, BANK], F32, name="unread")
         for i in range(WARMING_MATMULS):
-            nc.tensor.matmul(unread[:], averager[:], averager[:], start=True, stop=True)
+            nc.tensor.matmul(
+                unread[:], ones[:], ones[:, 0:1].to_broadcast([P, BANK]), start=True, stop=True
+            )
 
         scaled = held.tile([P, D_BLOCKS, N], BF16, name="scaled")
         squares = held.tile([P, D_BLOCKS, N], BF16, name="squares")

@@ -5,6 +5,7 @@ DIM, C, S, N = 256, 512, 512, 256
 D_BLOCKS = DIM // P
 C_BLOCKS = C // P
 EPS = 1e-05
+PAIR = 2 * P
 HALF = N // 2
 BANK = 512
 WARMING_MATMULS = 4
@@ -23,21 +24,28 @@ def tile_pagedtransformerblock_kernel(tc, x, nw, wkv, base, offs, out):
         tc.tile_pool(name="held", bufs=1) as held,
         tc.psum_pool(name="psum", bufs=1) as psum,
     ):
+        first, second = [slice(h * HALF, (h + 1) * HALF) for h in range(2)]
+        x_all = held.tile([P, D_BLOCKS, N], F32, name="x_all")
+        x_rows = x.rearrange("(p k) j -> p k j", p=P)
+        nc.sync.dma_start(x_all[:, :, first], x_rows[:, :, first])
+
         gain = held.tile([P, D_BLOCKS], F32, name="gain")
         nc.sync.dma_start(gain[:], nw.rearrange("(p k) o -> p (k o)", p=P))
 
-        x_all = held.tile([P, D_BLOCKS, N], F32, name="x_all")
-        nc.sync.dma_start(x_all[:], x.rearrange("(p k) j -> p k j", p=P))
-        x_blocks = [x_all[:, k, :] for k in range(D_BLOCKS)]
+        nc.sync.dma_start(x_all[:, :, second], x_rows[:, :, second])
 
-        weights = held.tile([P, D_BLOCKS, C], BF16, name="weights")
-        nc.sync.dma_start(weights[:], wkv.rearrange("(p k) c -> p k c", p=P))
+        weights = [held.tile([P, D_BLOCKS, PAIR], BF16, name=f"weights{h}") for h in range(2)]
+        wkv_rows = wkv.rearrange("(p k) c -> p k c", p=P)
+        nc.sync.dma_start(weights[0][:], wkv_rows[:, :, 0:PAIR])
 
         offsets = held.tile([P, N // 16], U16, name="offsets")
         nc.sync.dma_start(offsets[:], offs)
 
         windows = [held.tile([P, S], F32, name=f"window{b}") for b in range(C_BLOCKS)]
-        for b in range(C_BLOCKS):
+        for b in (0, 1):
+            nc.sync.dma_start(windows[b][:], base[b * P : (b + 1) * P, :])
+        nc.sync.dma_start(weights[1][:], wkv_rows[:, :, PAIR:C])
+        for b in (2, 3):
             nc.sync.dma_start(windows[b][:], base[b * P : (b + 1) * P, :])
 
         eps = held.tile([P, 1], F32, name="eps")
@@ -59,7 +67,7 @@ def tile_pagedtransformerblock_kernel(tc, x, nw, wkv, base, offs, out):
         scaled = held.tile([P, D_BLOCKS, N], BF16, name="scaled")
         squares = held.tile([P, D_BLOCKS, N], BF16, name="squares")
         r = held.tile([P, N], F32, name="r")
-        halves = [slice(h * HALF, (h + 1) * HALF) for h in range(2)]
+        halves = [first, second]
 
         def scale(tokens):
             for k in range(D_BLOCKS):
@@ -84,7 +92,7 @@ def tile_pagedtransformerblock_kernel(tc, x, nw, wkv, base, offs, out):
             for k in range(D_BLOCKS):
                 nc.tensor.matmul(
                     p[:],
-                    weights[:, k, b * P : (b + 1) * P],
+                    weights[b // 2][:, k, (b % 2) * P : (b % 2 + 1) * P],
                     scaled[:, k, tokens],
                     start=(k == 0),
                     stop=(k == D_BLOCKS - 1),
@@ -105,7 +113,6 @@ def tile_pagedtransformerblock_kernel(tc, x, nw, wkv, base, offs, out):
         def store(b):
             nc.sync.dma_start(out[b * P : (b + 1) * P, :], windows[b][:])
 
-        first, second = halves
         nc.scalar.activation(squares[:, 1, first], x_all[:, 1, first], ACT.Square)
         nc.vector.tensor_tensor(squares[:, 0, first], x_all[:, 0, first], x_all[:, 0, first], MULT)
         scale(first)
@@ -113,13 +120,11 @@ def tile_pagedtransformerblock_kernel(tc, x, nw, wkv, base, offs, out):
         scatter_half(0, project("0a", 0, first, HALF, "bank_0a"))
 
         scale(second)
-        nc.scalar.activation(squares[:, :, second], x_all[:, :, second], ACT.Square)
+        nc.vector.tensor_tensor(squares[:, :, second], x_all[:, :, second], x_all[:, :, second], MULT)
         normalise(1)
 
-        for b in (1, 2):
+        for b in range(1, C_BLOCKS):
             scatter_block(b, project(f"{b}", b, slice(0, N), N, f"bank_{b}"))
             store(b)
-        scatter_half(1, project("0b", 0, second, HALF, "bank_2"))
+        scatter_half(1, project("0b", 0, second, HALF, "bank_3"))
         store(0)
-        scatter_block(3, project("3", 3, slice(0, N), N, "bank_3"))
-        store(3)

import concourse.mybir as mybir

P = 128
DIM, C, S, N = 256, 512, 512, 256
D_BLOCKS = DIM // P
C_BLOCKS = C // P
EPS = 1e-05
PAIR = 2 * P
HALF = N // 2
BANK = 512
WARMING_MATMULS = 4
WARM_ROWS = 32

FLOPS = 2 * DIM * C * N + 2 * DIM * N

F32, BF16, U16 = mybir.dt.float32, mybir.dt.bfloat16, mybir.dt.uint16
ACT = mybir.ActivationFunctionType
MULT = mybir.AluOpType.mult


def tile_pagedtransformerblock_kernel(tc, x, nw, wkv, base, offs, out):
    nc = tc.nc
    with (
        tc.tile_pool(name="held", bufs=1) as held,
        tc.psum_pool(name="psum", bufs=1) as psum,
    ):
        first, second = [slice(h * HALF, (h + 1) * HALF) for h in range(2)]
        x_all = held.tile([P, D_BLOCKS, N], F32, name="x_all")
        x_rows = x.rearrange("(p k) j -> p k j", p=P)
        nc.sync.dma_start(x_all[:, :, first], x_rows[:, :, first])

        gain = held.tile([P, D_BLOCKS], F32, name="gain")
        nc.sync.dma_start(gain[:], nw.rearrange("(p k) o -> p (k o)", p=P))

        nc.sync.dma_start(x_all[:, :, second], x_rows[:, :, second])

        weights = [held.tile([P, D_BLOCKS, PAIR], BF16, name=f"weights{h}") for h in range(2)]
        wkv_rows = wkv.rearrange("(p k) c -> p k c", p=P)
        nc.sync.dma_start(weights[0][:], wkv_rows[:, :, 0:PAIR])

        offsets = held.tile([P, N // 16], U16, name="offsets")
        nc.sync.dma_start(offsets[:], offs)

        windows = [held.tile([P, S], F32, name=f"window{b}") for b in range(C_BLOCKS)]
        for b in (0, 1):
            nc.sync.dma_start(windows[b][:], base[b * P : (b + 1) * P, :])
        nc.sync.dma_start(weights[1][:], wkv_rows[:, :, PAIR:C])
        for b in (2, 3):
            nc.sync.dma_start(windows[b][:], base[b * P : (b + 1) * P, :])

        eps = held.tile([P, 1], F32, name="eps")
        nc.vector.memset(eps[:], EPS)
        averager = held.tile([P, P], BF16, name="averager")
        nc.vector.memset(averager[:], 1.0 / DIM)

        warm = held.tile([P, 1], F32, name="warm")
        nc.scalar.activation(warm[:], eps[:], ACT.Abs_reciprocal_sqrt)

        ones = held.tile([P, WARM_ROWS], BF16, name="ones")
        nc.gpsimd.memset(ones[:], 1.0)
        unread = psum.tile([WARM_ROWS, BANK], F32, name="unread")
        for i in range(WARMING_MATMULS):
            nc.tensor.matmul(
                unread[:], ones[:], ones[:, 0:1].to_broadcast([P, BANK]), start=True, stop=True
            )

        scaled = held.tile([P, D_BLOCKS, N], BF16, name="scaled")
        squares = held.tile([P, D_BLOCKS, N], BF16, name="squares")
        r = held.tile([P, N], F32, name="r")
        halves = [first, second]

        def scale(tokens):
            for k in range(D_BLOCKS):
                nc.vector.tensor_scalar_mul(
                    scaled[:, k, tokens], x_all[:, k, tokens], gain[:, k : k + 1]
                )

        def normalise(h):
            mean_sq = psum.tile([P, HALF], F32, name=f"mean_sq{h}")
            for k in range(D_BLOCKS):
                nc.tensor.matmul(
                    mean_sq[:],
                    averager[:],
                    squares[:, k, halves[h]],
                    start=(k == 0),
                    stop=(k == D_BLOCKS - 1),
                )
            nc.scalar.activation(r[:, halves[h]], mean_sq[:], ACT.Abs_reciprocal_sqrt, bias=eps[:])

        def project(name, b, tokens, columns, bank):
            p = psum.tile([P, columns], F32, name=f"p_{name}", tag=bank)
            for k in range(D_BLOCKS):
                nc.tensor.matmul(
                    p[:],
                    weights[b // 2][:, k, (b % 2) * P : (b % 2 + 1) * P],
                    scaled[:, k, tokens],
                    start=(k == 0),
                    stop=(k == D_BLOCKS - 1),
                )
            product = held.tile([P, columns], F32, name=f"product_{name}")
            nc.scalar.copy(product[:], p[:])
            return product

        def scatter_half(h, product):
            lists = slice(h * HALF // 16, (h + 1) * HALF // 16)
            nc.vector.tensor_tensor(
                windows[0][:].indirect(offsets[:, lists]), product[:], r[:, halves[h]], MULT
            )

        def scatter_block(b, product):
            nc.vector.tensor_tensor(windows[b][:].indirect(offsets[:]), product[:], r[:], MULT)

        def store(b):
            nc.sync.dma_start(out[b * P : (b + 1) * P, :], windows[b][:])

        nc.scalar.activation(squares[:, 1, first], x_all[:, 1, first], ACT.Square)
        nc.vector.tensor_tensor(squares[:, 0, first], x_all[:, 0, first], x_all[:, 0, first], MULT)
        scale(first)
        normalise(0)
        scatter_half(0, project("0a", 0, first, HALF, "bank_0a"))

        scale(second)
        nc.vector.tensor_tensor(squares[:, :, second], x_all[:, :, second], x_all[:, :, second], MULT)
        normalise(1)

        for b in range(1, C_BLOCKS):
            scatter_block(b, project(f"{b}", b, slice(0, N), N, f"bank_{b}"))
            store(b)
        scatter_half(1, project("0b", 0, second, HALF, "bank_3"))
        store(0)
